import numpy as np
import ml_dtypes


def mxq(x, axis, fmt="e4m3"):
    dtype, down = {"e4m3": (ml_dtypes.float8_e4m3fn, 7), "e5m2": (ml_dtypes.float8_e5m2, 14)}[fmt]
    v = np.moveaxis(np.asarray(x, np.float32).astype(ml_dtypes.bfloat16).astype(np.float64), axis, -1)
    blocks = v.reshape(v.shape[:-1] + (-1, 32))
    amax = np.abs(blocks).max(-1, keepdims=True)
    byte = np.maximum(np.where(amax > 0, np.frexp(amax)[1] - 1 + 127, 0) - down, 1)
    scale = np.exp2(byte - 127.0)
    codes = (blocks / scale).astype(np.float32).astype(dtype).astype(np.float64)
    return np.moveaxis((codes * scale).reshape(v.shape), -1, axis)


WIDE = False


def mx_kscale(k):
    if not WIDE:
        return np.ones(k)
    levels = np.array([10, -10, 5, -5, 0])
    if k % 512:
        return np.exp2(np.random.permutation(np.resize(levels, k // 32))).repeat(32)
    a = np.empty((k // 512, 16))
    for p in range(k // 512):
        a[p, :8] = np.random.permutation(np.resize(levels, 8))
        for g in range(8):
            far = levels[np.abs(levels - a[p, g]) >= 10]
            a[p, g + 8] = far[np.random.randint(len(far))]
    return np.exp2(a.ravel()).repeat(32)


BF16 = ml_dtypes.bfloat16


def bf(x):
    return np.asarray(x, np.float32).astype(BF16)


def f64(x):
    return np.asarray(x).astype(np.float64)


B, S, HID, H, HKV, DH = 4, 2048, 512, 2, 1, 64
NH = H + 2 * HKV


def rotate_half(x):
    x1 = x[..., ::2]
    x2 = x[..., 1::2]
    return np.stack((-x2, x1), axis=-1).reshape(x.shape)


def setup_inputs():
    s = mx_kscale(HID)
    inv_freq = 1.0 / (10000.0 ** (np.arange(0, DH, 2) / DH))
    emb = np.repeat(np.outer(np.arange(S), inv_freq), 2, axis=-1)
    return {"hidden_states": bf(np.random.standard_normal((B, S, HID)) * s),
            "cos": bf(np.cos(emb)),
            "sin": bf(np.sin(emb)),
            "w_qkv": bf(np.random.standard_normal((NH * DH, HID)) / np.sqrt(HID) / s[None, :])}


def reference(hidden_states, cos, sin, w_qkv):
    qkv = mxq(f64(hidden_states), 2, "e4m3") @ mxq(f64(w_qkv), 1, "e4m3").T
    qkv = qkv.reshape(B, S, NH, DH)
    q = qkv[:, :, :H]
    k = qkv[:, :, H:H + HKV]
    v = qkv[:, :, H + HKV:]
    cos_s = f64(cos)[:S][None, :, None, :]
    sin_s = f64(sin)[:S][None, :, None, :]
    q = q * cos_s + rotate_half(q) * sin_s
    k = k * cos_s + rotate_half(k) * sin_s
    return q, k, v

@@ -1,0 +1,205 @@
+from contextlib import ExitStack
+
+import concourse.mybir as mybir
+from concourse.masks import make_identity
+
+F32 = mybir.dt.float32
+BF16 = mybir.dt.bfloat16
+U32 = mybir.dt.uint32
+U8 = mybir.dt.uint8
+FP8X4 = mybir.dt.float8_e4m3fn_x4
+MULT = mybir.AluOpType.mult
+ADD = mybir.AluOpType.add
+
+P = 128
+B, S, HID = 4, 2048, 512
+DH = 64
+TPB = S // P
+GT = 4
+NG = B * TPB // GT
+FLOPS = 2 * B * S * HID * 256
+
+LOADS = [(0, 0, 4), (0, 4, 4), (0, 8, 8), (1, 0, 16), (2, 0, 16), (3, 0, 16)]
+STORES = [(0, 0, 8), (0, 8, 8), (1, 0, 8), (1, 8, 8), (2, 0, 8), (2, 8, 8), (3, 0, 8), (3, 8, 4), (3, 12, 4)]
+V_ADD_Q = (15,)
+V_ADD_K = (3, 7, 11, 14, 15)
+
+
+def tile_attention_pa_t_kernel(tc, hidden_states, cos, sin, w_qkv, out_0, out_1, out_2):
+    nc = tc.nc
+    with ExitStack() as ctx:
+        const = ctx.enter_context(tc.tile_pool(name="const", bufs=1))
+        xin = ctx.enter_context(tc.tile_pool(name="xin", bufs=1))
+        outp = ctx.enter_context(tc.tile_pool(name="outp", bufs=1))
+        gp = ctx.enter_context(tc.tile_pool(name="gp", bufs=3))
+        cp = ctx.enter_context(tc.tile_pool(name="cp", bufs=2))
+        pp = ctx.enter_context(tc.tile_pool(name="pp", bufs=3))
+        tpp = ctx.enter_context(tc.psum_pool(name="tpp", bufs=4))
+        mmp = ctx.enter_context(tc.psum_pool(name="mmp", bufs=4))
+        ctx.enter_context(tc.manual_schedule())
+
+        ident = const.tile([P, P], F32, name="ident")
+        make_identity(nc, ident[:])
+        perm = const.tile([P, P], F32, name="perm")
+        w_sb = const.tile([P, 2, HID], BF16, name="w_sb")
+        tab = const.tile([P, 2, TPB, DH], BF16, name="tab")
+
+        nc.sync.dma_start(out=w_sb[:], in_=w_qkv.rearrange("(a p) k -> p a k", p=P))
+        x_of = {}
+        x_tiles = []
+        for (b, t0, n) in LOADS:
+            xt = xin.tile([P, n, HID], BF16, name="x%d_%d" % (b, t0))
+            x_tiles.append((xt, b, t0, n))
+            for l0 in range(0, n, GT):
+                x_of[(b * TPB + t0 + l0) // GT] = (xt, l0)
+
+        def load_x(i):
+            xt, b, t0, n = x_tiles[i]
+            nc.sync.dma_start(
+                out=xt[:],
+                in_=hidden_states[b].rearrange("(p t) k -> p t k", t=TPB)[:, t0:t0 + n, :],
+            )
+
+        load_x(0)
+        load_x(1)
+        nc.sync.dma_start(out=tab[:, 1], in_=sin.rearrange("(p t) j -> p t j", t=TPB))
+        nc.sync.dma_start(out=tab[:, 0], in_=cos.rearrange("(p t) j -> p t j", t=TPB))
+        for i in range(2, len(LOADS)):
+            load_x(i)
+
+        out_of = {}
+        for (b, t0, n) in STORES:
+            q_sb = outp.tile([P, n, 2 * DH], F32, name="q%d_%d" % (b, t0))
+            k_sb = outp.tile([P, n, DH], F32, name="k%d_%d" % (b, t0))
+            v_sb = outp.tile([P, n, DH], F32, name="v%d_%d" % (b, t0))
+            for l0 in range(0, n, GT):
+                out_of[(b * TPB + t0 + l0) // GT] = (q_sb, k_sb, v_sb, l0, l0 + GT == n, b, t0, n)
+
+        iv = ident[:].rearrange("p (n e) -> p n e", e=2)
+        pv = perm[:].rearrange("p (n e) -> p n e", e=2)
+        nc.vector.tensor_copy(out=pv[:, :, 0], in_=iv[:, :, 1])
+        nc.vector.tensor_copy(out=pv[:, :, 1], in_=iv[:, :, 0])
+
+        def evac(eng_is_vector, dst, bank):
+            src = bank[:].rearrange("p a u r -> p a r u")
+            if eng_is_vector:
+                nc.vector.tensor_copy(out=dst, in_=src)
+            else:
+                nc.scalar.copy(out=dst, in_=src)
+
+        banks_of = {}
+        grp_of = {}
+        code_of = {}
+        mm_of = {}
+        p_of = {}
+
+        def stage_t(g):
+            xt, l0 = x_of[g]
+            xw = xt[:].bitcast(F32)
+            banks = []
+            for h in range(2):
+                tp = tpp.tile([P, 2, 2, P], F32, name="tp", tag="tp")
+                for a in range(2):
+                    for u in range(2):
+                        nc.tensor.transpose(tp[:, a, u, :], xw[:, l0 + 2 * h + a, u:2 * P:2], ident[:])
+                banks.append(tp)
+            banks_of[g] = banks
+
+        def stage_e(g, second_on_vector=False):
+            grp = gp.tile([P, GT, P, 4], BF16, name="grp", tag="grp", align_bytes=64)
+            banks = banks_of[g]
+            evac(False, grp[:, 0:2].bitcast(F32), banks[0])
+            evac(second_on_vector, grp[:, 2:4].bitcast(F32), banks[1])
+            grp_of[g] = grp
+
+        def stage_q(g):
+            codes = cp.tile([P, GT * P], U32, name="codes", tag="codes", align_bytes=64)
+            scl = cp.tile([P, GT * P], U8, name="scl", tag="scl", align_bytes=64)
+            nc.vector.quantize_mx(
+                out=codes[:].bitcast(FP8X4),
+                scales=scl[:],
+                in_=grp_of[g][:].rearrange("p a r t -> p (a r t)"),
+            )
+            code_of[g] = (codes, scl)
+
+        def stage_m(g, i):
+            codes, scl = code_of[g]
+            mm = mmp.tile([P, 512], F32, name="mm", tag="mm")
+            nc.tensor.matmul_mx(
+                out=mm[:],
+                lhsT=codes[:, P * i:P * (i + 1)].bitcast(FP8X4),
+                lhsT_scale=scl[:, P * i:P * (i + 1)],
+                rhs=w_codes[:].bitcast(FP8X4),
+                rhs_scale=w_scl[:],
+                start=True,
+                stop=True,
+            )
+            mm_of[(g, i)] = mm
+            v_sb, l0 = out_of[g][2], out_of[g][3]
+            nc.scalar.copy(out=v_sb[:, l0 + i, :], in_=mm[:, 3 * DH:4 * DH])
+
+        def stage_x(g, i):
+            if i == 0:
+                p_of[g] = pp.tile([P, GT, 2, 3 * DH], F32, name="prod", tag="prod")
+            t = (g * GT + i) % TPB
+            nc.vector.tensor_tensor(
+                out=p_of[g][:, i].rearrange("p c (h j) -> p c h j", h=3),
+                in0=mm_of[(g, i)][:].rearrange("p (c h j) -> p c h j", c=2, h=4)[:, :, 0:3, :],
+                in1=tab[:, :, t, :].unsqueeze(2).to_broadcast([P, 2, 3, DH]),
+                op=MULT,
+            )
+
+        def stage_a(g):
+            q_sb, k_sb, v_sb, l0, last, b, t0, n = out_of[g]
+            prod = p_of[g]
+            eq = nc.vector if g in V_ADD_Q else nc.gpsimd
+            ek = nc.vector if g in V_ADD_K else nc.gpsimd
+            eq.tensor_tensor(out=q_sb[:, l0:l0 + GT, :], in0=prod[:, :, 0, 0:2 * DH], in1=prod[:, :, 1, 0:2 * DH], op=ADD)
+            ek.tensor_tensor(out=k_sb[:, l0:l0 + GT, :], in0=prod[:, :, 0, 2 * DH:3 * DH], in1=prod[:, :, 1, 2 * DH:3 * DH], op=ADD)
+            if last:
+                nc.sync.dma_start(out=out_2[b].rearrange("(p t) h j -> p t (h j)", t=TPB)[:, t0:t0 + n, :], in_=v_sb[:])
+                nc.sync.dma_start(out=out_0[b].rearrange("(p t) h j -> p t (h j)", t=TPB)[:, t0:t0 + n, :], in_=q_sb[:])
+                nc.sync.dma_start(out=out_1[b].rearrange("(p t) h j -> p t (h j)", t=TPB)[:, t0:t0 + n, :], in_=k_sb[:])
+
+        ww = w_sb[:].bitcast(F32)
+        w_grp = const.tile([P, 4, P, 4], BF16, name="w_grp", align_bytes=64)
+        w_codes = const.tile([P, 512], U32, name="w_codes", align_bytes=64)
+        w_scl = const.tile([P, 512], U8, name="w_scl", align_bytes=64)
+        w_banks = []
+        for mat in (ident, perm):
+            tp = tpp.tile([P, 2, 2, P], F32, name="tp", tag="tp")
+            for a in range(2):
+                for u in range(2):
+                    nc.tensor.transpose(tp[:, a, u, :], ww[:, a, u:2 * P:2], mat[:])
+            w_banks.append(tp)
+        evac(False, w_grp[:, 0:2].bitcast(F32), w_banks[0])
+        evac(True, w_grp[:, 2:4].bitcast(F32), w_banks[1])
+        stage_t(0)
+        nc.vector.quantize_mx(
+            out=w_codes[:].bitcast(FP8X4),
+            scales=w_scl[:],
+            in_=w_grp[:].rearrange("p a r t -> p (a r t)"),
+        )
+        stage_e(0, second_on_vector=True)
+        stage_t(1)
+        stage_q(0)
+        stage_e(1)
+        sv = tab[:, 1].rearrange("p t (i e) -> p (t i) e", e=2)[:, :, 0]
+        nc.vector.tensor_scalar_mul(out=sv, in0=sv, scalar1=-1.0)
+        for i in range(GT):
+            stage_m(0, i)
+        stage_t(2)
+        stage_e(2)
+
+        for k in range(NG):
+            if k + 3 < NG:
+                stage_t(k + 3)
+            if k + 1 < NG:
+                stage_q(k + 1)
+            if k + 3 < NG:
+                stage_e(k + 3)
+            for i in range(GT):
+                stage_x(k, i)
+                if k + 1 < NG:
+                    stage_m(k + 1, i)
+            stage_a(k)

@@ -21,8 +21,7 @@ FLOPS = 2 * B * S * HID * 256
 
 LOADS = [(0, 0, 4), (0, 4, 4), (0, 8, 8), (1, 0, 16), (2, 0, 16), (3, 0, 16)]
 STORES = [(0, 0, 8), (0, 8, 8), (1, 0, 8), (1, 8, 8), (2, 0, 8), (2, 8, 8), (3, 0, 8), (3, 8, 4), (3, 12, 4)]
-V_ADD_Q = (15,)
-V_ADD_K = (3, 7, 11, 14, 15)
+V_ADD = (15,)
 
 
 def tile_attention_pa_t_kernel(tc, hidden_states, cos, sin, w_qkv, out_0, out_1, out_2):
@@ -69,11 +68,10 @@ def tile_attention_pa_t_kernel(tc, hidden_states, cos, sin, w_qkv, out_0, out_1,
 
         out_of = {}
         for (b, t0, n) in STORES:
-            q_sb = outp.tile([P, n, 2 * DH], F32, name="q%d_%d" % (b, t0))
-            k_sb = outp.tile([P, n, DH], F32, name="k%d_%d" % (b, t0))
+            qk_sb = outp.tile([P, n, 3 * DH], F32, name="qk%d_%d" % (b, t0))
             v_sb = outp.tile([P, n, DH], F32, name="v%d_%d" % (b, t0))
             for l0 in range(0, n, GT):
-                out_of[(b * TPB + t0 + l0) // GT] = (q_sb, k_sb, v_sb, l0, l0 + GT == n, b, t0, n)
+                out_of[(b * TPB + t0 + l0) // GT] = (qk_sb, v_sb, l0, l0 + GT == n, b, t0, n)
 
         iv = ident[:].rearrange("p (n e) -> p n e", e=2)
         pv = perm[:].rearrange("p (n e) -> p n e", e=2)
@@ -135,7 +133,7 @@ def tile_attention_pa_t_kernel(tc, hidden_states, cos, sin, w_qkv, out_0, out_1,
                 stop=True,
             )
             mm_of[(g, i)] = mm
-            v_sb, l0 = out_of[g][2], out_of[g][3]
+            v_sb, l0 = out_of[g][1], out_of[g][2]
             nc.scalar.copy(out=v_sb[:, l0 + i, :], in_=mm[:, 3 * DH:4 * DH])
 
         def stage_x(g, i):
@@ -150,16 +148,14 @@ def tile_attention_pa_t_kernel(tc, hidden_states, cos, sin, w_qkv, out_0, out_1,
             )
 
         def stage_a(g):
-            q_sb, k_sb, v_sb, l0, last, b, t0, n = out_of[g]
+            qk_sb, v_sb, l0, last, b, t0, n = out_of[g]
             prod = p_of[g]
-            eq = nc.vector if g in V_ADD_Q else nc.gpsimd
-            ek = nc.vector if g in V_ADD_K else nc.gpsimd
-            eq.tensor_tensor(out=q_sb[:, l0:l0 + GT, :], in0=prod[:, :, 0, 0:2 * DH], in1=prod[:, :, 1, 0:2 * DH], op=ADD)
-            ek.tensor_tensor(out=k_sb[:, l0:l0 + GT, :], in0=prod[:, :, 0, 2 * DH:3 * DH], in1=prod[:, :, 1, 2 * DH:3 * DH], op=ADD)
+            eng = nc.vector if g in V_ADD else nc.gpsimd
+            eng.tensor_tensor(out=qk_sb[:, l0:l0 + GT, :], in0=prod[:, :, 0, :], in1=prod[:, :, 1, :], op=ADD)
             if last:
                 nc.sync.dma_start(out=out_2[b].rearrange("(p t) h j -> p t (h j)", t=TPB)[:, t0:t0 + n, :], in_=v_sb[:])
-                nc.sync.dma_start(out=out_0[b].rearrange("(p t) h j -> p t (h j)", t=TPB)[:, t0:t0 + n, :], in_=q_sb[:])
-                nc.sync.dma_start(out=out_1[b].rearrange("(p t) h j -> p t (h j)", t=TPB)[:, t0:t0 + n, :], in_=k_sb[:])
+                nc.sync.dma_start(out=out_0[b].rearrange("(p t) h j -> p t (h j)", t=TPB)[:, t0:t0 + n, :], in_=qk_sb[:, :, 0:2 * DH])
+                nc.sync.dma_start(out=out_1[b].rearrange("(p t) h j -> p t (h j)", t=TPB)[:, t0:t0 + n, :], in_=qk_sb[:, :, 2 * DH:3 * DH])
 
         ww = w_sb[:].bitcast(F32)
         w_grp = const.tile([P, 4, P, 4], BF16, name="w_grp", align_bytes=64)

@@ -19,9 +19,8 @@ GT = 4
 NG = B * TPB // GT
 FLOPS = 2 * B * S * HID * 256
 
-LOADS = [(0, 0, 4), (0, 4, 4), (0, 8, 8), (1, 0, 16), (2, 0, 16), (3, 0, 16)]
+LOADS = [(0, 0, 4), (0, 4, 4), (0, 8, 4), (0, 12, 4), (1, 0, 4), (1, 4, 4), (1, 8, 8), (2, 0, 8), (2, 8, 8), (3, 0, 16)]
 STORES = [(0, 0, 8), (0, 8, 8), (1, 0, 8), (1, 8, 8), (2, 0, 8), (2, 8, 8), (3, 0, 8), (3, 8, 4), (3, 12, 4)]
-V_ADD = (15,)
 
 
 def tile_attention_pa_t_kernel(tc, hidden_states, cos, sin, w_qkv, out_0, out_1, out_2):
@@ -68,10 +67,17 @@ def tile_attention_pa_t_kernel(tc, hidden_states, cos, sin, w_qkv, out_0, out_1,
 
         out_of = {}
         for (b, t0, n) in STORES:
-            qk_sb = outp.tile([P, n, 3 * DH], F32, name="qk%d_%d" % (b, t0))
+            if n > GT:
+                qk_sb = outp.tile([P, n, 3 * DH], F32, name="qk%d_%d" % (b, t0))
+                q_view, k_view = qk_sb[:, :, 0:2 * DH], qk_sb[:, :, 2 * DH:3 * DH]
+            else:
+                qk_sb = None
+                q_sb = outp.tile([P, n, 2 * DH], F32, name="q%d_%d" % (b, t0))
+                k_sb = outp.tile([P, n, DH], F32, name="k%d_%d" % (b, t0))
+                q_view, k_view = q_sb[:], k_sb[:]
             v_sb = outp.tile([P, n, DH], F32, name="v%d_%d" % (b, t0))
             for l0 in range(0, n, GT):
-                out_of[(b * TPB + t0 + l0) // GT] = (qk_sb, v_sb, l0, l0 + GT == n, b, t0, n)
+                out_of[(b * TPB + t0 + l0) // GT] = (qk_sb, v_sb, l0, l0 + GT == n, b, t0, n, q_view, k_view)
 
         iv = ident[:].rearrange("p (n e) -> p n e", e=2)
         pv = perm[:].rearrange("p (n e) -> p n e", e=2)
@@ -103,22 +109,23 @@ def tile_attention_pa_t_kernel(tc, hidden_states, cos, sin, w_qkv, out_0, out_1,
                 banks.append(tp)
             banks_of[g] = banks
 
-        def stage_e(g, second_on_vector=False):
-            grp = gp.tile([P, GT, P, 4], BF16, name="grp", tag="grp", align_bytes=64)
-            banks = banks_of[g]
-            evac(False, grp[:, 0:2].bitcast(F32), banks[0])
-            evac(second_on_vector, grp[:, 2:4].bitcast(F32), banks[1])
-            grp_of[g] = grp
+        def stage_e(g, halves=(0, 1), on_vector=False):
+            for h in halves:
+                if h == 0:
+                    grp_of[g] = gp.tile([P, GT, P, 4], BF16, name="grp", tag="grp", align_bytes=64)
+                evac(on_vector, grp_of[g][:, 2 * h:2 * h + 2].bitcast(F32), banks_of[g][h])
 
-        def stage_q(g):
-            codes = cp.tile([P, GT * P], U32, name="codes", tag="codes", align_bytes=64)
-            scl = cp.tile([P, GT * P], U8, name="scl", tag="scl", align_bytes=64)
+        def stage_q(g, a0=0, na=GT):
+            if a0 == 0:
+                codes = cp.tile([P, GT * P], U32, name="codes", tag="codes", align_bytes=64)
+                scl = cp.tile([P, GT * P], U8, name="scl", tag="scl", align_bytes=64)
+                code_of[g] = (codes, scl)
+            codes, scl = code_of[g]
             nc.vector.quantize_mx(
-                out=codes[:].bitcast(FP8X4),
-                scales=scl[:],
-                in_=grp_of[g][:].rearrange("p a r t -> p (a r t)"),
+                out=codes[:, P * a0:P * (a0 + na)].bitcast(FP8X4),
+                scales=scl[:, P * a0:P * (a0 + na)],
+                in_=grp_of[g][:, a0:a0 + na].rearrange("p a r t -> p (a r t)"),
             )
-            code_of[g] = (codes, scl)
 
         def stage_m(g, i):
             codes, scl = code_of[g]
@@ -147,15 +154,25 @@ def tile_attention_pa_t_kernel(tc, hidden_states, cos, sin, w_qkv, out_0, out_1,
                 op=MULT,
             )
 
-        def stage_a(g):
-            qk_sb, v_sb, l0, last, b, t0, n = out_of[g]
+        def stage_a2(eng, g, a0, na, eng_k=None):
+            qk_sb, v_sb, l0, last, b, t0, n, q_view, k_view = out_of[g]
             prod = p_of[g]
-            eng = nc.vector if g in V_ADD else nc.gpsimd
-            eng.tensor_tensor(out=qk_sb[:, l0:l0 + GT, :], in0=prod[:, :, 0, :], in1=prod[:, :, 1, :], op=ADD)
+            eng.tensor_tensor(out=q_view[:, l0 + a0:l0 + a0 + na, :], in0=prod[:, a0:a0 + na, 0, 0:2 * DH], in1=prod[:, a0:a0 + na, 1, 0:2 * DH], op=ADD)
+            (eng_k or eng).tensor_tensor(out=k_view[:, l0 + a0:l0 + a0 + na, :], in0=prod[:, a0:a0 + na, 0, 2 * DH:3 * DH], in1=prod[:, a0:a0 + na, 1, 2 * DH:3 * DH], op=ADD)
+
+        def stage_a(g):
+            qk_sb, v_sb, l0, last, b, t0, n, q_view, k_view = out_of[g]
+            prod = p_of[g]
+            if qk_sb is not None:
+                nc.gpsimd.tensor_tensor(out=qk_sb[:, l0:l0 + GT, :], in0=prod[:, :, 0, :], in1=prod[:, :, 1, :], op=ADD)
+            elif g < NG - 1:
+                stage_a2(nc.gpsimd, g, 0, GT, eng_k=nc.vector)
+            else:
+                stage_a2(nc.vector, g, 2, 2)
             if last:
                 nc.sync.dma_start(out=out_2[b].rearrange("(p t) h j -> p t (h j)", t=TPB)[:, t0:t0 + n, :], in_=v_sb[:])
-                nc.sync.dma_start(out=out_0[b].rearrange("(p t) h j -> p t (h j)", t=TPB)[:, t0:t0 + n, :], in_=qk_sb[:, :, 0:2 * DH])
-                nc.sync.dma_start(out=out_1[b].rearrange("(p t) h j -> p t (h j)", t=TPB)[:, t0:t0 + n, :], in_=qk_sb[:, :, 2 * DH:3 * DH])
+                nc.sync.dma_start(out=out_0[b].rearrange("(p t) h j -> p t (h j)", t=TPB)[:, t0:t0 + n, :], in_=q_view)
+                nc.sync.dma_start(out=out_1[b].rearrange("(p t) h j -> p t (h j)", t=TPB)[:, t0:t0 + n, :], in_=k_view)
 
         ww = w_sb[:].bitcast(F32)
         w_grp = const.tile([P, 4, P, 4], BF16, name="w_grp", align_bytes=64)
@@ -176,26 +193,35 @@ def tile_attention_pa_t_kernel(tc, hidden_states, cos, sin, w_qkv, out_0, out_1,
             scales=w_scl[:],
             in_=w_grp[:].rearrange("p a r t -> p (a r t)"),
         )
-        stage_e(0, second_on_vector=True)
-        stage_t(1)
-        stage_q(0)
-        stage_e(1)
         sv = tab[:, 1].rearrange("p t (i e) -> p (t i) e", e=2)[:, :, 0]
-        nc.vector.tensor_scalar_mul(out=sv, in0=sv, scalar1=-1.0)
-        for i in range(GT):
-            stage_m(0, i)
+        nc.gpsimd.tensor_scalar(out=sv, in0=sv, scalar1=-1.0, scalar2=0.0, op0=MULT, op1=ADD)
+        stage_e(0)
+        stage_t(1)
+        stage_q(0, 0, 2)
+        stage_m(0, 0)
+        stage_m(0, 1)
+        stage_q(0, 2, 2)
+        stage_e(1, halves=(0,), on_vector=True)
+        stage_e(1, halves=(1,))
+        stage_m(0, 2)
+        stage_m(0, 3)
         stage_t(2)
         stage_e(2)
 
         for k in range(NG):
             if k + 3 < NG:
                 stage_t(k + 3)
-            if k + 1 < NG:
+            if 0 < k < NG - 1:
                 stage_q(k + 1)
             if k + 3 < NG:
                 stage_e(k + 3)
             for i in range(GT):
                 stage_x(k, i)
-                if k + 1 < NG:
+                if k == 0 and i == 1:
+                    stage_q(1)
+                    stage_m(1, 0)
+                if k + 1 < NG and (k > 0 or i > 0):
                     stage_m(k + 1, i)
+                if k == NG - 1 and i == 1:
+                    stage_a2(nc.gpsimd, k, 0, 2)
             stage_a(k)

@@ -38,7 +38,6 @@ def tile_attention_pa_t_kernel(tc, hidden_states, cos, sin, w_qkv, out_0, out_1,
 
         ident = const.tile([P, P], F32, name="ident")
         make_identity(nc, ident[:])
-        perm = const.tile([P, P], F32, name="perm")
         w_sb = const.tile([P, 2, HID], BF16, name="w_sb")
         tab = const.tile([P, 2, TPB, DH], BF16, name="tab")
 
@@ -79,10 +78,6 @@ def tile_attention_pa_t_kernel(tc, hidden_states, cos, sin, w_qkv, out_0, out_1,
             for l0 in range(0, n, GT):
                 out_of[(b * TPB + t0 + l0) // GT] = (qk_sb, v_sb, l0, l0 + GT == n, b, t0, n, q_view, k_view)
 
-        iv = ident[:].rearrange("p (n e) -> p n e", e=2)
-        pv = perm[:].rearrange("p (n e) -> p n e", e=2)
-        nc.vector.tensor_copy(out=pv[:, :, 0], in_=iv[:, :, 1])
-        nc.vector.tensor_copy(out=pv[:, :, 1], in_=iv[:, :, 0])
 
         def evac(eng_is_vector, dst, bank):
             src = bank[:].rearrange("p a u r -> p a r u")
@@ -127,30 +122,39 @@ def tile_attention_pa_t_kernel(tc, hidden_states, cos, sin, w_qkv, out_0, out_1,
                 in_=grp_of[g][:, a0:a0 + na].rearrange("p a r t -> p (a r t)"),
             )
 
-        def stage_m(g, i):
+        def stage_m(g, h):
             codes, scl = code_of[g]
-            mm = mmp.tile([P, 512], F32, name="mm", tag="mm")
-            nc.tensor.matmul_mx(
-                out=mm[:],
-                lhsT=codes[:, P * i:P * (i + 1)].bitcast(FP8X4),
-                lhsT_scale=scl[:, P * i:P * (i + 1)],
-                rhs=w_codes[:].bitcast(FP8X4),
-                rhs_scale=w_scl[:],
-                start=True,
-                stop=True,
-            )
-            mm_of[(g, i)] = mm
+            mm = mmp.tile([P, 2, 256], F32, name="mm", tag="mm")
+            for a in range(2):
+                i = 2 * h + a
+                nc.tensor.matmul_mx(
+                    out=mm[:, a, :],
+                    lhsT=codes[:, P * i:P * (i + 1)].bitcast(FP8X4),
+                    lhsT_scale=scl[:, P * i:P * (i + 1)],
+                    rhs=w_codes[:].bitcast(FP8X4),
+                    rhs_scale=w_scl[:],
+                    start=True,
+                    stop=True,
+                )
+            mm_of[(g, h)] = mm
             v_sb, l0 = out_of[g][1], out_of[g][2]
-            nc.scalar.copy(out=v_sb[:, l0 + i, :], in_=mm[:, 3 * DH:4 * DH])
+            nc.scalar.copy(out=v_sb[:, l0 + 2 * h:l0 + 2 * h + 2, :], in_=mm[:, :, 3 * DH:4 * DH])
 
-        def stage_x(g, i):
-            if i == 0:
+        def stage_x(g, h):
+            if h == 0:
                 p_of[g] = pp.tile([P, GT, 2, 3 * DH], F32, name="prod", tag="prod")
-            t = (g * GT + i) % TPB
+            t = (g * GT + 2 * h) % TPB
+            qk = mm_of[(g, h)][:, :, 0:3 * DH]
             nc.vector.tensor_tensor(
-                out=p_of[g][:, i].rearrange("p c (h j) -> p c h j", h=3),
-                in0=mm_of[(g, i)][:].rearrange("p (c h j) -> p c h j", c=2, h=4)[:, :, 0:3, :],
-                in1=tab[:, :, t, :].unsqueeze(2).to_broadcast([P, 2, 3, DH]),
+                out=p_of[g][:, 2 * h:2 * h + 2, 0, :].rearrange("p a (h j) -> p a h j", h=3),
+                in0=qk.rearrange("p a (h j) -> p a h j", h=3),
+                in1=tab[:, 0, t:t + 2, :].unsqueeze(2).to_broadcast([P, 2, 3, DH]),
+                op=MULT,
+            )
+            nc.vector.tensor_tensor(
+                out=p_of[g][:, 2 * h:2 * h + 2, 1, :].rearrange("p a (h i e) -> p a h i e", h=3, e=2),
+                in0=qk.rearrange("p a (h i e) -> p a h i e", h=3, e=2)[:, :, :, :, ::-1],
+                in1=tab[:, 1, t:t + 2, :].rearrange("p a (i e) -> p a i e", e=2).unsqueeze(2).to_broadcast([P, 2, 3, DH // 2, 2]),
                 op=MULT,
             )
 
@@ -175,18 +179,14 @@ def tile_attention_pa_t_kernel(tc, hidden_states, cos, sin, w_qkv, out_0, out_1,
                 nc.sync.dma_start(out=out_1[b].rearrange("(p t) h j -> p t (h j)", t=TPB)[:, t0:t0 + n, :], in_=k_view)
 
         ww = w_sb[:].bitcast(F32)
-        w_grp = const.tile([P, 4, P, 4], BF16, name="w_grp", align_bytes=64)
-        w_codes = const.tile([P, 512], U32, name="w_codes", align_bytes=64)
-        w_scl = const.tile([P, 512], U8, name="w_scl", align_bytes=64)
-        w_banks = []
-        for mat in (ident, perm):
-            tp = tpp.tile([P, 2, 2, P], F32, name="tp", tag="tp")
-            for a in range(2):
-                for u in range(2):
-                    nc.tensor.transpose(tp[:, a, u, :], ww[:, a, u:2 * P:2], mat[:])
-            w_banks.append(tp)
-        evac(False, w_grp[:, 0:2].bitcast(F32), w_banks[0])
-        evac(True, w_grp[:, 2:4].bitcast(F32), w_banks[1])
+        w_grp = const.tile([P, 2, P, 4], BF16, name="w_grp", align_bytes=64)
+        w_codes = const.tile([P, 256], U32, name="w_codes", align_bytes=64)
+        w_scl = const.tile([P, 256], U8, name="w_scl", align_bytes=64)
+        wtp = tpp.tile([P, 2, 2, P], F32, name="tp", tag="tp")
+        for a in range(2):
+            for u in range(2):
+                nc.tensor.transpose(wtp[:, a, u, :], ww[:, a, u:2 * P:2], ident[:])
+        evac(True, w_grp[:].bitcast(F32), wtp)
         stage_t(0)
         nc.vector.quantize_mx(
             out=w_codes[:].bitcast(FP8X4),
@@ -199,12 +199,10 @@ def tile_attention_pa_t_kernel(tc, hidden_states, cos, sin, w_qkv, out_0, out_1,
         stage_t(1)
         stage_q(0, 0, 2)
         stage_m(0, 0)
-        stage_m(0, 1)
         stage_q(0, 2, 2)
         stage_e(1, halves=(0,), on_vector=True)
         stage_e(1, halves=(1,))
-        stage_m(0, 2)
-        stage_m(0, 3)
+        stage_m(0, 1)
         stage_t(2)
         stage_e(2)
 
@@ -215,13 +213,12 @@ def tile_attention_pa_t_kernel(tc, hidden_states, cos, sin, w_qkv, out_0, out_1,
                 stage_q(k + 1)
             if k + 3 < NG:
                 stage_e(k + 3)
-            for i in range(GT):
-                stage_x(k, i)
-                if k == 0 and i == 1:
+            for h in range(2):
+                stage_x(k, h)
+                if k == 0 and h == 0:
                     stage_q(1)
-                    stage_m(1, 0)
-                if k + 1 < NG and (k > 0 or i > 0):
-                    stage_m(k + 1, i)
-                if k == NG - 1 and i == 1:
+                if k + 1 < NG:
+                    stage_m(k + 1, h)
+                if k == NG - 1 and h == 0:
                     stage_a2(nc.gpsimd, k, 0, 2)
             stage_a(k)

@@ -18,8 +18,9 @@ TPB = S // P
 GT = 4
 NG = B * TPB // GT
 FLOPS = 2 * B * S * HID * 256
+WARM = 3
 
-LOADS = [(0, 0, 4), (0, 4, 4), (0, 8, 4), (0, 12, 4), (1, 0, 4), (1, 4, 4), (1, 8, 8), (2, 0, 8), (2, 8, 8), (3, 0, 16)]
+LOADS = [(0, 0, 2), (0, 2, 2), (0, 4, 4), (0, 8, 4), (0, 12, 4), (1, 0, 4), (1, 4, 4), (1, 8, 8), (2, 0, 8), (2, 8, 8), (3, 0, 16)]
 STORES = [(0, 0, 8), (0, 8, 8), (1, 0, 8), (1, 8, 8), (2, 0, 8), (2, 8, 8), (3, 0, 8), (3, 8, 4), (3, 12, 4)]
 
 
@@ -36,6 +37,12 @@ def tile_attention_pa_t_kernel(tc, hidden_states, cos, sin, w_qkv, out_0, out_1,
         mmp = ctx.enter_context(tc.psum_pool(name="mmp", bufs=4))
         ctx.enter_context(tc.manual_schedule())
 
+        zeros = const.tile([P, 512], BF16, name="zeros")
+        nc.gpsimd.memset(zeros[:], 0.0)
+        warm = mmp.tile([P, 2, 256], F32, name="mm", tag="mm")
+        for i in range(WARM):
+            nc.tensor.matmul(warm[:].rearrange("p a c -> p (a c)"), lhsT=zeros[:, 0:P], rhs=zeros[:], start=True, stop=True)
+
         ident = const.tile([P, P], F32, name="ident")
         make_identity(nc, ident[:])
         w_sb = const.tile([P, 2, HID], BF16, name="w_sb")
@@ -47,8 +54,8 @@ def tile_attention_pa_t_kernel(tc, hidden_states, cos, sin, w_qkv, out_0, out_1,
         for (b, t0, n) in LOADS:
             xt = xin.tile([P, n, HID], BF16, name="x%d_%d" % (b, t0))
             x_tiles.append((xt, b, t0, n))
-            for l0 in range(0, n, GT):
-                x_of[(b * TPB + t0 + l0) // GT] = (xt, l0)
+            for l0 in range(0, n, 2):
+                x_of[(b * TPB + t0 + l0) // 2] = (xt, l0)
 
         def load_x(i):
             xt, b, t0, n = x_tiles[i]
@@ -59,9 +66,10 @@ def tile_attention_pa_t_kernel(tc, hidden_states, cos, sin, w_qkv, out_0, out_1,
 
         load_x(0)
         load_x(1)
+        load_x(2)
         nc.sync.dma_start(out=tab[:, 1], in_=sin.rearrange("(p t) j -> p t j", t=TPB))
         nc.sync.dma_start(out=tab[:, 0], in_=cos.rearrange("(p t) j -> p t j", t=TPB))
-        for i in range(2, len(LOADS)):
+        for i in range(3, len(LOADS)):
             load_x(i)
 
         out_of = {}
@@ -93,14 +101,14 @@ def tile_attention_pa_t_kernel(tc, hidden_states, cos, sin, w_qkv, out_0, out_1,
         p_of = {}
 
         def stage_t(g):
-            xt, l0 = x_of[g]
-            xw = xt[:].bitcast(F32)
             banks = []
             for h in range(2):
+                xt, l0 = x_of[2 * g + h]
+                xw = xt[:].bitcast(F32)
                 tp = tpp.tile([P, 2, 2, P], F32, name="tp", tag="tp")
                 for a in range(2):
                     for u in range(2):
-                        nc.tensor.transpose(tp[:, a, u, :], xw[:, l0 + 2 * h + a, u:2 * P:2], ident[:])
+                        nc.tensor.transpose(tp[:, a, u, :], xw[:, l0 + a, u:2 * P:2], ident[:])
                 banks.append(tp)
             banks_of[g] = banks
 
@@ -137,8 +145,12 @@ def tile_attention_pa_t_kernel(tc, hidden_states, cos, sin, w_qkv, out_0, out_1,
                     stop=True,
                 )
             mm_of[(g, h)] = mm
+            if g > 0:
+                stage_v(g, h)
+
+        def stage_v(g, h):
             v_sb, l0 = out_of[g][1], out_of[g][2]
-            nc.scalar.copy(out=v_sb[:, l0 + 2 * h:l0 + 2 * h + 2, :], in_=mm[:, :, 3 * DH:4 * DH])
+            nc.scalar.copy(out=v_sb[:, l0 + 2 * h:l0 + 2 * h + 2, :], in_=mm_of[(g, h)][:, :, 3 * DH:4 * DH])
 
         def stage_x(g, h):
             if h == 0:
@@ -176,7 +188,8 @@ def tile_attention_pa_t_kernel(tc, hidden_states, cos, sin, w_qkv, out_0, out_1,
             if last:
                 nc.sync.dma_start(out=out_2[b].rearrange("(p t) h j -> p t (h j)", t=TPB)[:, t0:t0 + n, :], in_=v_sb[:])
                 nc.sync.dma_start(out=out_0[b].rearrange("(p t) h j -> p t (h j)", t=TPB)[:, t0:t0 + n, :], in_=q_view)
-                nc.sync.dma_start(out=out_1[b].rearrange("(p t) h j -> p t (h j)", t=TPB)[:, t0:t0 + n, :], in_=k_view)
+                k_queue = nc.scalar if g == NG - 1 else nc.sync
+                k_queue.dma_start(out=out_1[b].rearrange("(p t) h j -> p t (h j)", t=TPB)[:, t0:t0 + n, :], in_=k_view)
 
         ww = w_sb[:].bitcast(F32)
         w_grp = const.tile([P, 2, P, 4], BF16, name="w_grp", align_bytes=64)
@@ -207,18 +220,23 @@ def tile_attention_pa_t_kernel(tc, hidden_states, cos, sin, w_qkv, out_0, out_1,
         stage_e(2)
 
         for k in range(NG):
-            if k + 3 < NG:
+            if 0 < k < NG - 3:
                 stage_t(k + 3)
             if 0 < k < NG - 1:
                 stage_q(k + 1)
-            if k + 3 < NG:
+            if 0 < k < NG - 3:
                 stage_e(k + 3)
             for h in range(2):
                 stage_x(k, h)
+                if k == 0:
+                    stage_v(0, h)
                 if k == 0 and h == 0:
                     stage_q(1)
                 if k + 1 < NG:
                     stage_m(k + 1, h)
                 if k == NG - 1 and h == 0:
                     stage_a2(nc.gpsimd, k, 0, 2)
+            if k == 0:
+                stage_t(3)
+                stage_e(3)
             stage_a(k)

from contextlib import ExitStack

import concourse.mybir as mybir
from concourse.masks import make_identity

F32 = mybir.dt.float32
BF16 = mybir.dt.bfloat16
U32 = mybir.dt.uint32
U8 = mybir.dt.uint8
FP8X4 = mybir.dt.float8_e4m3fn_x4
MULT = mybir.AluOpType.mult
ADD = mybir.AluOpType.add

P = 128
B, S, HID = 4, 2048, 512
DH = 64
TPB = S // P
GT = 4
NG = B * TPB // GT
FLOPS = 2 * B * S * HID * 256
WARM = 3

LOADS = [(0, 0, 2), (0, 2, 2), (0, 4, 4), (0, 8, 4), (0, 12, 4), (1, 0, 4), (1, 4, 4), (1, 8, 8), (2, 0, 8), (2, 8, 8), (3, 0, 16)]
STORES = [(0, 0, 8), (0, 8, 8), (1, 0, 8), (1, 8, 8), (2, 0, 8), (2, 8, 8), (3, 0, 8), (3, 8, 4), (3, 12, 4)]


def tile_attention_pa_t_kernel(tc, hidden_states, cos, sin, w_qkv, out_0, out_1, out_2):
    nc = tc.nc
    with ExitStack() as ctx:
        const = ctx.enter_context(tc.tile_pool(name="const", bufs=1))
        xin = ctx.enter_context(tc.tile_pool(name="xin", bufs=1))
        outp = ctx.enter_context(tc.tile_pool(name="outp", bufs=1))
        gp = ctx.enter_context(tc.tile_pool(name="gp", bufs=3))
        cp = ctx.enter_context(tc.tile_pool(name="cp", bufs=2))
        pp = ctx.enter_context(tc.tile_pool(name="pp", bufs=3))
        tpp = ctx.enter_context(tc.psum_pool(name="tpp", bufs=4))
        mmp = ctx.enter_context(tc.psum_pool(name="mmp", bufs=4))
        ctx.enter_context(tc.manual_schedule())

        zeros = const.tile([P, 512], BF16, name="zeros")
        nc.gpsimd.memset(zeros[:], 0.0)
        warm = mmp.tile([P, 2, 256], F32, name="mm", tag="mm")
        for i in range(WARM):
            nc.tensor.matmul(warm[:].rearrange("p a c -> p (a c)"), lhsT=zeros[:, 0:P], rhs=zeros[:], start=True, stop=True)

        ident = const.tile([P, P], F32, name="ident")
        make_identity(nc, ident[:])
        w_sb = const.tile([P, 2, HID], BF16, name="w_sb")
        tab = const.tile([P, 2, TPB, DH], BF16, name="tab")

        nc.sync.dma_start(out=w_sb[:], in_=w_qkv.rearrange("(a p) k -> p a k", p=P))
        x_of = {}
        x_tiles = []
        for (b, t0, n) in LOADS:
            xt = xin.tile([P, n, HID], BF16, name="x%d_%d" % (b, t0))
            x_tiles.append((xt, b, t0, n))
            for l0 in range(0, n, 2):
                x_of[(b * TPB + t0 + l0) // 2] = (xt, l0)

        def load_x(i):
            xt, b, t0, n = x_tiles[i]
            nc.sync.dma_start(
                out=xt[:],
                in_=hidden_states[b].rearrange("(p t) k -> p t k", t=TPB)[:, t0:t0 + n, :],
            )

        load_x(0)
        load_x(1)
        load_x(2)
        nc.sync.dma_start(out=tab[:, 1], in_=sin.rearrange("(p t) j -> p t j", t=TPB))
        nc.sync.dma_start(out=tab[:, 0], in_=cos.rearrange("(p t) j -> p t j", t=TPB))
        for i in range(3, len(LOADS)):
            load_x(i)

        out_of = {}
        for (b, t0, n) in STORES:
            if n > GT:
                qk_sb = outp.tile([P, n, 3 * DH], F32, name="qk%d_%d" % (b, t0))
                q_view, k_view = qk_sb[:, :, 0:2 * DH], qk_sb[:, :, 2 * DH:3 * DH]
            else:
                qk_sb = None
                q_sb = outp.tile([P, n, 2 * DH], F32, name="q%d_%d" % (b, t0))
                k_sb = outp.tile([P, n, DH], F32, name="k%d_%d" % (b, t0))
                q_view, k_view = q_sb[:], k_sb[:]
            v_sb = outp.tile([P, n, DH], F32, name="v%d_%d" % (b, t0))
            for l0 in range(0, n, GT):
                out_of[(b * TPB + t0 + l0) // GT] = (qk_sb, v_sb, l0, l0 + GT == n, b, t0, n, q_view, k_view)


        def evac(eng_is_vector, dst, bank):
            src = bank[:].rearrange("p a u r -> p a r u")
            if eng_is_vector:
                nc.vector.tensor_copy(out=dst, in_=src)
            else:
                nc.scalar.copy(out=dst, in_=src)

        banks_of = {}
        grp_of = {}
        code_of = {}
        mm_of = {}
        p_of = {}

        def stage_t(g):
            banks = []
            for h in range(2):
                xt, l0 = x_of[2 * g + h]
                xw = xt[:].bitcast(F32)
                tp = tpp.tile([P, 2, 2, P], F32, name="tp", tag="tp")
                for a in range(2):
                    for u in range(2):
                        nc.tensor.transpose(tp[:, a, u, :], xw[:, l0 + a, u:2 * P:2], ident[:])
                banks.append(tp)
            banks_of[g] = banks

        def stage_e(g, halves=(0, 1), on_vector=False):
            for h in halves:
                if h == 0:
                    grp_of[g] = gp.tile([P, GT, P, 4], BF16, name="grp", tag="grp", align_bytes=64)
                evac(on_vector, grp_of[g][:, 2 * h:2 * h + 2].bitcast(F32), banks_of[g][h])

        def stage_q(g, a0=0, na=GT):
            if a0 == 0:
                codes = cp.tile([P, GT * P], U32, name="codes", tag="codes", align_bytes=64)
                scl = cp.tile([P, GT * P], U8, name="scl", tag="scl", align_bytes=64)
                code_of[g] = (codes, scl)
            codes, scl = code_of[g]
            nc.vector.quantize_mx(
                out=codes[:, P * a0:P * (a0 + na)].bitcast(FP8X4),
                scales=scl[:, P * a0:P * (a0 + na)],
                in_=grp_of[g][:, a0:a0 + na].rearrange("p a r t -> p (a r t)"),
            )

        def stage_m(g, h):
            codes, scl = code_of[g]
            mm = mmp.tile([P, 2, 256], F32, name="mm", tag="mm")
            for a in range(2):
                i = 2 * h + a
                nc.tensor.matmul_mx(
                    out=mm[:, a, :],
                    lhsT=codes[:, P * i:P * (i + 1)].bitcast(FP8X4),
                    lhsT_scale=scl[:, P * i:P * (i + 1)],
                    rhs=w_codes[:].bitcast(FP8X4),
                    rhs_scale=w_scl[:],
                    start=True,
                    stop=True,
                )
            mm_of[(g, h)] = mm
            if g > 0:
                stage_v(g, h)

        def stage_v(g, h):
            v_sb, l0 = out_of[g][1], out_of[g][2]
            nc.scalar.copy(out=v_sb[:, l0 + 2 * h:l0 + 2 * h + 2, :], in_=mm_of[(g, h)][:, :, 3 * DH:4 * DH])

        def stage_x(g, h):
            if h == 0:
                p_of[g] = pp.tile([P, GT, 2, 3 * DH], F32, name="prod", tag="prod")
            t = (g * GT + 2 * h) % TPB
            qk = mm_of[(g, h)][:, :, 0:3 * DH]
            nc.vector.tensor_tensor(
                out=p_of[g][:, 2 * h:2 * h + 2, 0, :].rearrange("p a (h j) -> p a h j", h=3),
                in0=qk.rearrange("p a (h j) -> p a h j", h=3),
                in1=tab[:, 0, t:t + 2, :].unsqueeze(2).to_broadcast([P, 2, 3, DH]),
                op=MULT,
            )
            nc.vector.tensor_tensor(
                out=p_of[g][:, 2 * h:2 * h + 2, 1, :].rearrange("p a (h i e) -> p a h i e", h=3, e=2),
                in0=qk.rearrange("p a (h i e) -> p a h i e", h=3, e=2)[:, :, :, :, ::-1],
                in1=tab[:, 1, t:t + 2, :].rearrange("p a (i e) -> p a i e", e=2).unsqueeze(2).to_broadcast([P, 2, 3, DH // 2, 2]),
                op=MULT,
            )

        def stage_a2(eng, g, a0, na, eng_k=None):
            qk_sb, v_sb, l0, last, b, t0, n, q_view, k_view = out_of[g]
            prod = p_of[g]
            eng.tensor_tensor(out=q_view[:, l0 + a0:l0 + a0 + na, :], in0=prod[:, a0:a0 + na, 0, 0:2 * DH], in1=prod[:, a0:a0 + na, 1, 0:2 * DH], op=ADD)
            (eng_k or eng).tensor_tensor(out=k_view[:, l0 + a0:l0 + a0 + na, :], in0=prod[:, a0:a0 + na, 0, 2 * DH:3 * DH], in1=prod[:, a0:a0 + na, 1, 2 * DH:3 * DH], op=ADD)

        def stage_a(g):
            qk_sb, v_sb, l0, last, b, t0, n, q_view, k_view = out_of[g]
            prod = p_of[g]
            if qk_sb is not None:
                nc.gpsimd.tensor_tensor(out=qk_sb[:, l0:l0 + GT, :], in0=prod[:, :, 0, :], in1=prod[:, :, 1, :], op=ADD)
            elif g < NG - 1:
                stage_a2(nc.gpsimd, g, 0, GT, eng_k=nc.vector)
            else:
                stage_a2(nc.vector, g, 2, 2)
            if last:
                nc.sync.dma_start(out=out_2[b].rearrange("(p t) h j -> p t (h j)", t=TPB)[:, t0:t0 + n, :], in_=v_sb[:])
                nc.sync.dma_start(out=out_0[b].rearrange("(p t) h j -> p t (h j)", t=TPB)[:, t0:t0 + n, :], in_=q_view)
                k_queue = nc.scalar if g == NG - 1 else nc.sync
                k_queue.dma_start(out=out_1[b].rearrange("(p t) h j -> p t (h j)", t=TPB)[:, t0:t0 + n, :], in_=k_view)

        ww = w_sb[:].bitcast(F32)
        w_grp = const.tile([P, 2, P, 4], BF16, name="w_grp", align_bytes=64)
        w_codes = const.tile([P, 256], U32, name="w_codes", align_bytes=64)
        w_scl = const.tile([P, 256], U8, name="w_scl", align_bytes=64)
        wtp = tpp.tile([P, 2, 2, P], F32, name="tp", tag="tp")
        for a in range(2):
            for u in range(2):
                nc.tensor.transpose(wtp[:, a, u, :], ww[:, a, u:2 * P:2], ident[:])
        evac(True, w_grp[:].bitcast(F32), wtp)
        stage_t(0)
        nc.vector.quantize_mx(
            out=w_codes[:].bitcast(FP8X4),
            scales=w_scl[:],
            in_=w_grp[:].rearrange("p a r t -> p (a r t)"),
        )
        sv = tab[:, 1].rearrange("p t (i e) -> p (t i) e", e=2)[:, :, 0]
        nc.gpsimd.tensor_scalar(out=sv, in0=sv, scalar1=-1.0, scalar2=0.0, op0=MULT, op1=ADD)
        stage_e(0)
        stage_t(1)
        stage_q(0, 0, 2)
        stage_m(0, 0)
        stage_q(0, 2, 2)
        stage_e(1, halves=(0,), on_vector=True)
        stage_e(1, halves=(1,))
        stage_m(0, 1)
        stage_t(2)
        stage_e(2)

        for k in range(NG):
            if 0 < k < NG - 3:
                stage_t(k + 3)
            if 0 < k < NG - 1:
                stage_q(k + 1)
            if 0 < k < NG - 3:
                stage_e(k + 3)
            for h in range(2):
                stage_x(k, h)
                if k == 0:
                    stage_v(0, h)
                if k == 0 and h == 0:
                    stage_q(1)
                if k + 1 < NG:
                    stage_m(k + 1, h)
                if k == NG - 1 and h == 0:
                    stage_a2(nc.gpsimd, k, 0, 2)
            if k == 0:
                stage_t(3)
                stage_e(3)
            stage_a(k)
